import numpy as np
import ml_dtypes


def mxq(x, axis, fmt="e4m3"):
    dtype, down = {"e4m3": (ml_dtypes.float8_e4m3fn, 7), "e5m2": (ml_dtypes.float8_e5m2, 14)}[fmt]
    v = np.moveaxis(np.asarray(x, np.float32).astype(ml_dtypes.bfloat16).astype(np.float64), axis, -1)
    blocks = v.reshape(v.shape[:-1] + (-1, 32))
    amax = np.abs(blocks).max(-1, keepdims=True)
    byte = np.maximum(np.where(amax > 0, np.frexp(amax)[1] - 1 + 127, 0) - down, 1)
    scale = np.exp2(byte - 127.0)
    codes = (blocks / scale).astype(np.float32).astype(dtype).astype(np.float64)
    return np.moveaxis((codes * scale).reshape(v.shape), -1, axis)


WIDE = False


def mx_kscale(k):
    if not WIDE:
        return np.ones(k)
    levels = np.array([10, -10, 5, -5, 0])
    a = np.random.permutation(np.resize(levels, k // 512 * 4)).reshape(k // 512, 4)
    idx = np.arange(k)
    return np.exp2(a[idx // 512, idx % 128 // 32])


BF16 = ml_dtypes.bfloat16


def bf(x):
    return np.asarray(x, np.float32).astype(BF16)


def f64(x):
    return np.asarray(x).astype(np.float64)


T, H, I, R = 4096, 512, 128, 512


def silu(v):
    return v / (1.0 + np.exp(-v))


def setup_inputs():
    s, t = mx_kscale(H), mx_kscale(R)
    return {
        "x": bf(np.random.standard_normal((T, H)) * s),
        "Wmean1": bf(np.random.standard_normal((I, H)) / np.sqrt(H) / s),
        "Wmean3": bf(np.random.standard_normal((I, H)) / np.sqrt(H) / s),
        "du1": bf(np.random.standard_normal((I, R)) * 0.5 / np.sqrt(R) / t),
        "dv1": bf(np.random.standard_normal((R, H)) / np.sqrt(H) / s * t[:, None]),
        "du3": bf(np.random.standard_normal((I, R)) * 0.5 / np.sqrt(R) / t),
        "dv3": bf(np.random.standard_normal((R, H)) / np.sqrt(H) / s * t[:, None]),
    }


def reference(x, Wmean1, Wmean3, du1, dv1, du3, dv3):
    xq = mxq(f64(x), 1, "e4m3")
    p3 = xq @ mxq(f64(dv3), 1, "e4m3").T
    up = (xq @ mxq(f64(Wmean3), 1, "e4m3").T) + (mxq(p3, 1, "e4m3") @ mxq(f64(du3), 1, "e4m3").T)
    p1 = xq @ mxq(f64(dv1), 1, "e4m3").T
    gate = (xq @ mxq(f64(Wmean1), 1, "e4m3").T) + (mxq(p1, 1, "e4m3") @ mxq(f64(du1), 1, "e4m3").T)
    return silu(gate) * up

@@ -1,0 +1,228 @@
+from contextlib import ExitStack
+
+import concourse.masks as masks
+import concourse.mybir as mybir
+
+F32 = mybir.dt.float32
+BF16 = mybir.dt.bfloat16
+U32 = mybir.dt.uint32
+U8 = mybir.dt.uint8
+FP8X4 = mybir.dt.float8_e4m3fn_x4
+ACT = mybir.ActivationFunctionType
+ALU = mybir.AluOpType
+
+T, H, I, R = 4096, 512, 128, 512
+P = 128
+BLOCK = 512
+NB = T // BLOCK
+FLOPS = 2 * T * (2 * H * R + 2 * H * I + 2 * R * I)
+
+
+def tile_merge_mixtralsparsemoeblock_pa_t_kernel(tc, x, Wmean1, Wmean3, du1, dv1, du3, dv3, out):
+    nc = tc.nc
+    x_blocks = x.rearrange("(b p n) h -> b p (n h)", p=P, n=4)
+    out_blocks = out.rearrange("(b p n) i -> b p (n i)", p=P, n=4)
+
+    with ExitStack() as ctx:
+        const = ctx.enter_context(tc.tile_pool(name="const", bufs=1))
+        work = ctx.enter_context(tc.tile_pool(name="work", bufs=2))
+        psum = ctx.enter_context(tc.psum_pool(name="psum", bufs=2))
+        ctx.enter_context(tc.manual_schedule())
+
+        def copy_on(engine, dst, src):
+            if engine == "act":
+                nc.scalar.copy(out=dst, in_=src)
+            else:
+                nc.vector.tensor_copy(out=dst, in_=src)
+
+        def bank(tag, bufs):
+            return psum.tile([P, 512], F32, name=tag, tag=tag, bufs=bufs)
+
+        def transpose4(tag, bufs, sources):
+            t = bank(tag, bufs)
+            for k, src in enumerate(sources):
+                nc.tensor.transpose(t[:, 128 * k : 128 * k + 128], src, ident[:])
+            return t
+
+        def interleave(engine, dst_bf16, t):
+            copy_on(
+                engine,
+                dst_bf16.bitcast(F32).rearrange("q (a c u) -> q a c u", a=2, u=2),
+                t[:].rearrange("q (a u c) -> q a c u", a=2, u=2),
+            )
+
+        def quantise(codes, scales, src):
+            nc.vector.quantize_mx(out=codes[:].bitcast(FP8X4), scales=scales[:], in_=src[:])
+
+        ident = const.tile([P, P], F32, name="ident")
+        masks.make_identity(nc, ident[:])
+        warm_in = const.tile([P, 1], F32, name="warm_in")
+        warm_out = const.tile([P, 1], F32, name="warm_out")
+        nc.vector.memset(warm_in[:], 0.0)
+        nc.scalar.activation(out=warm_out[:], in_=warm_in[:], func=ACT.Silu)
+
+        x_sb = [const.tile([P, 2048], BF16, name="x_sb%d" % b) for b in range(NB)]
+        dv_sb = [const.tile([P, 2048], BF16, name="dv_sb%d" % w) for w in range(2)]
+        wm_sb = [const.tile([P, 512], BF16, name="wm_sb%d" % w) for w in range(2)]
+        du_sb = [const.tile([P, 512], BF16, name="du_sb%d" % w) for w in range(2)]
+        nc.sync.dma_start(out=x_sb[0][:, 0:1024], in_=x_blocks[0][:, 0:1024])
+        nc.sync.dma_start(out=x_sb[0][:, 1024:2048], in_=x_blocks[0][:, 1024:2048])
+        nc.sync.dma_start(out=dv_sb[0][:], in_=dv3.rearrange("(m j) h -> m (j h)", j=4))
+        nc.sync.dma_start(out=dv_sb[1][:], in_=dv1.rearrange("(m j) h -> m (j h)", j=4))
+        nc.sync.dma_start(out=x_sb[1][:], in_=x_blocks[1])
+        nc.sync.dma_start(out=wm_sb[0][:], in_=Wmean3)
+        nc.sync.dma_start(out=wm_sb[1][:], in_=Wmean1)
+        nc.sync.dma_start(out=du_sb[0][:], in_=du3)
+        nc.sync.dma_start(out=du_sb[1][:], in_=du1)
+        for b in range(2, NB):
+            nc.sync.dma_start(out=x_sb[b][:], in_=x_blocks[b])
+
+        xq = [const.tile([P, 512], U32, name="xq%d" % b, align_bytes=64) for b in range(NB)]
+        xs = [const.tile([P, 512], U8, name="xs%d" % b, align_bytes=64) for b in range(NB)]
+        dvq = [const.tile([P, 512], U32, name="dvq%d" % w, align_bytes=64) for w in range(2)]
+        dvs = [const.tile([P, 512], U8, name="dvs%d" % w, align_bytes=64) for w in range(2)]
+        gd = [const.tile([P, 2048], BF16, name="gd%d" % w, align_bytes=64) for w in range(2)]
+        gw = const.tile([P, 2048], BF16, name="gw", align_bytes=64)
+        wq = const.tile([P, 512], U32, name="wq", align_bytes=64)
+        ws = const.tile([P, 512], U8, name="ws", align_bytes=64)
+        z = [const.tile([P, 512], F32, name="z%d" % b) for b in range(NB)]
+
+        state = {}
+
+        def tx(b):
+            xf = x_sb[b][:].bitcast(F32)
+            state["gx", b] = work.tile([P, 2048], BF16, name="gx", tag="gx", bufs=2, align_bytes=64)
+            for h in range(2):
+                state["xt", b, h] = transpose4(
+                    "xt", 2, [xf[:, 512 * h + 128 * k : 512 * h + 128 * k + 128] for k in range(4)]
+                )
+
+        def cx(b, h, engine):
+            interleave(engine, state["gx", b][:, 1024 * h : 1024 * h + 1024], state["xt", b, h])
+
+        def qx(b):
+            quantise(xq[b], xs[b], state["gx", b])
+
+        def s1(b, n, w):
+            t = bank("pb", 4)
+            state["pb", b, n, w] = t
+            for j in range(4):
+                nc.tensor.matmul_mx(
+                    out=t[:, 128 * j : 128 * j + 128],
+                    lhsT=dvq[w][:, 128 * j : 128 * j + 128].bitcast(FP8X4),
+                    lhsT_scale=dvs[w][:, 128 * j : 128 * j + 128],
+                    rhs=xq[b][:, 128 * n : 128 * n + 128].bitcast(FP8X4),
+                    rhs_scale=xs[b][:, 128 * n : 128 * n + 128],
+                    start=True,
+                    stop=True,
+                )
+
+        def cp(b, n, w, engine):
+            h, n2 = divmod(n, 2)
+            if ("gp", b, h) not in state:
+                state["gp", b, h] = work.tile([P, 2048], BF16, name="gp", tag="gp", bufs=4, align_bytes=64)
+            c = 512 * (2 * w + n2)
+            copy_on(
+                engine,
+                state["gp", b, h][:, c : c + 512].rearrange("m (t j) -> m t j", j=4),
+                state["pb", b, n, w][:].rearrange("m (j t) -> m t j", j=4),
+            )
+
+        def qp(b, h):
+            state["pq", b, h] = work.tile([P, 512], U32, name="pq", tag="pq", bufs=4, align_bytes=64)
+            state["ps", b, h] = work.tile([P, 512], U8, name="ps", tag="ps", bufs=4, align_bytes=64)
+            quantise(state["pq", b, h], state["ps", b, h], state["gp", b, h])
+
+        def s2(b, n):
+            h, n2 = divmod(n, 2)
+            if n2 == 0:
+                state["ob", b, h] = bank("ob", 2)
+            t = state["ob", b, h]
+            for w in range(2):
+                col = 256 * (1 - w) + 128 * n2
+                pc = 128 * (2 * w + n2)
+                nc.tensor.matmul_mx(
+                    out=t[:, col : col + 128],
+                    lhsT=xq[b][:, 128 * n : 128 * n + 128].bitcast(FP8X4),
+                    lhsT_scale=xs[b][:, 128 * n : 128 * n + 128],
+                    rhs=wq[:, 128 * w : 128 * w + 128].bitcast(FP8X4),
+                    rhs_scale=ws[:, 128 * w : 128 * w + 128],
+                    start=True,
+                    stop=False,
+                )
+                nc.tensor.matmul_mx(
+                    out=t[:, col : col + 128],
+                    lhsT=state["pq", b, h][:, pc : pc + 128].bitcast(FP8X4),
+                    lhsT_scale=state["ps", b, h][:, pc : pc + 128],
+                    rhs=wq[:, 256 + 128 * w : 256 + 128 * w + 128].bitcast(FP8X4),
+                    rhs_scale=ws[:, 256 + 128 * w : 256 + 128 * w + 128],
+                    start=False,
+                    stop=True,
+                )
+
+        def finish(b, h):
+            t = state["ob", b, h]
+            sg = work.tile([P, 256], F32, name="sg", tag="sg", bufs=3)
+            nc.scalar.activation(out=sg[:], in_=t[:, 0:256], func=ACT.Silu)
+            nc.vector.tensor_tensor(out=z[b][:, 256 * h : 256 * h + 256], in0=sg[:], in1=t[:, 256:512], op=ALU.mult)
+
+        tx(0)
+        cx(0, 0, "act")
+        cx(0, 1, "dve")
+        for w in range(2):
+            df = dv_sb[w][:].bitcast(F32)
+            for h in range(2):
+                state["dt", w, h] = transpose4(
+                    "pb", 4, [df[:, 512 * h + 128 * k : 512 * h + 128 * k + 128] for k in range(4)]
+                )
+            interleave("act", gd[w][:, 0:1024], state["dt", w, 0])
+            interleave("dve" if w == 0 else "act", gd[w][:, 1024:2048], state["dt", w, 1])
+            if w == 0:
+                qx(0)
+            else:
+                quantise(dvq[0], dvs[0], gd[0])
+        tx(1)
+        cx(1, 0, "act")
+        cx(1, 1, "dve")
+        quantise(dvq[1], dvs[1], gd[1])
+        wt = transpose4("ob", 2, [wm_sb[w][:].bitcast(F32)[:, 128 * u : 128 * u + 128] for w in range(2) for u in range(2)])
+        ut = transpose4(
+            "ob", 2,
+            [du_sb[w][:].bitcast(F32).rearrange("i (m u) -> i u m", u=2)[:, u, :] for w in range(2) for u in range(2)],
+        )
+        interleave("act", gw[:, 0:1024], wt)
+        interleave("act", gw[:, 1024:2048], ut)
+        qx(1)
+        quantise(wq, ws, gw)
+
+        for b in range(NB + 1):
+            ahead = 1 <= b and b + 1 < NB
+            if ahead:
+                tx(b + 1)
+            if b >= 2:
+                finish(b - 2, 1)
+                nc.sync.dma_start(out=out_blocks[b - 2], in_=z[b - 2][:])
+            if ahead:
+                cx(b + 1, 0, "act")
+                cx(b + 1, 1, "dve")
+            if b >= 1:
+                qp(b - 1, 1)
+            if ahead:
+                qx(b + 1)
+            for n in range(4):
+                if b < NB:
+                    s1(b, n, 0)
+                    cp(b, n, 0, "act")
+                    s1(b, n, 1)
+                    cp(b, n, 1, "dve" if n % 2 == 1 else "act")
+                if b >= 1:
+                    s2(b - 1, n)
+                if n == 1:
+                    if b >= 1:
+                        finish(b - 1, 0)
+                    if b < NB:
+                        qp(b, 0)
+                    else:
+                        nc.sync.dma_start(out=out_blocks[NB - 1][:, 0:256], in_=z[NB - 1][:, 0:256])
+        finish(NB - 1, 1)
+        nc.sync.dma_start(out=out_blocks[NB - 1][:, 256:512], in_=z[NB - 1][:, 256:512])

@@ -52,7 +52,7 @@ def tile_merge_mixtralsparsemoeblock_pa_t_kernel(tc, x, Wmean1, Wmean3, du1, dv1
             )
 
         def quantise(codes, scales, src):
-            nc.vector.quantize_mx(out=codes[:].bitcast(FP8X4), scales=scales[:], in_=src[:])
+            nc.vector.quantize_mx(out=codes.bitcast(FP8X4), scales=scales, in_=src)
 
         ident = const.tile([P, P], F32, name="ident")
         masks.make_identity(nc, ident[:])
@@ -65,16 +65,17 @@ def tile_merge_mixtralsparsemoeblock_pa_t_kernel(tc, x, Wmean1, Wmean3, du1, dv1
         dv_sb = [const.tile([P, 2048], BF16, name="dv_sb%d" % w) for w in range(2)]
         wm_sb = [const.tile([P, 512], BF16, name="wm_sb%d" % w) for w in range(2)]
         du_sb = [const.tile([P, 512], BF16, name="du_sb%d" % w) for w in range(2)]
+        dv3_rows = dv3.rearrange("(m j) h -> m (j h)", j=4)
+        nc.sync.dma_start(out=dv_sb[0][:, 0:1024], in_=dv3_rows[:, 0:1024])
+        nc.sync.dma_start(out=dv_sb[0][:, 1024:2048], in_=dv3_rows[:, 1024:2048])
         nc.sync.dma_start(out=x_sb[0][:, 0:1024], in_=x_blocks[0][:, 0:1024])
         nc.sync.dma_start(out=x_sb[0][:, 1024:2048], in_=x_blocks[0][:, 1024:2048])
-        nc.sync.dma_start(out=dv_sb[0][:], in_=dv3.rearrange("(m j) h -> m (j h)", j=4))
         nc.sync.dma_start(out=dv_sb[1][:], in_=dv1.rearrange("(m j) h -> m (j h)", j=4))
-        nc.sync.dma_start(out=x_sb[1][:], in_=x_blocks[1])
         nc.sync.dma_start(out=wm_sb[0][:], in_=Wmean3)
         nc.sync.dma_start(out=wm_sb[1][:], in_=Wmean1)
         nc.sync.dma_start(out=du_sb[0][:], in_=du3)
         nc.sync.dma_start(out=du_sb[1][:], in_=du1)
-        for b in range(2, NB):
+        for b in range(1, NB):
             nc.sync.dma_start(out=x_sb[b][:], in_=x_blocks[b])
 
         xq = [const.tile([P, 512], U32, name="xq%d" % b, align_bytes=64) for b in range(NB)]
@@ -101,7 +102,14 @@ def tile_merge_mixtralsparsemoeblock_pa_t_kernel(tc, x, Wmean1, Wmean3, du1, dv1
             interleave(engine, state["gx", b][:, 1024 * h : 1024 * h + 1024], state["xt", b, h])
 
         def qx(b):
-            quantise(xq[b], xs[b], state["gx", b])
+            quantise(xq[b][:], xs[b][:], state["gx", b][:])
+
+        def qx_half(b, h):
+            quantise(
+                xq[b][:, 256 * h : 256 * h + 256],
+                xs[b][:, 256 * h : 256 * h + 256],
+                state["gx", b][:, 1024 * h : 1024 * h + 1024],
+            )
 
         def s1(b, n, w):
             t = bank("pb", 4)
@@ -121,26 +129,44 @@ def tile_merge_mixtralsparsemoeblock_pa_t_kernel(tc, x, Wmean1, Wmean3, du1, dv1
             h, n2 = divmod(n, 2)
             if ("gp", b, h) not in state:
                 state["gp", b, h] = work.tile([P, 2048], BF16, name="gp", tag="gp", bufs=4, align_bytes=64)
-            c = 512 * (2 * w + n2)
+            c = 512 * (2 * n2 + w)
             copy_on(
                 engine,
                 state["gp", b, h][:, c : c + 512].rearrange("m (t j) -> m t j", j=4),
                 state["pb", b, n, w][:].rearrange("m (j t) -> m t j", j=4),
             )
 
-        def qp(b, h):
-            state["pq", b, h] = work.tile([P, 512], U32, name="pq", tag="pq", bufs=4, align_bytes=64)
-            state["ps", b, h] = work.tile([P, 512], U8, name="ps", tag="ps", bufs=4, align_bytes=64)
-            quantise(state["pq", b, h], state["ps", b, h], state["gp", b, h])
+        def p_words(b, h):
+            if ("pq", b, h) not in state:
+                state["pq", b, h] = work.tile([P, 512], U32, name="pq", tag="pq", bufs=4, align_bytes=64)
+                state["ps", b, h] = work.tile([P, 512], U8, name="ps", tag="ps", bufs=4, align_bytes=64)
+            return state["pq", b, h], state["ps", b, h]
 
-        def s2(b, n):
+        def qp(b, h):
+            codes, scales = p_words(b, h)
+            quantise(codes[:], scales[:], state["gp", b, h][:])
+
+        def qp_tile(b, n):
             h, n2 = divmod(n, 2)
-            if n2 == 0:
-                state["ob", b, h] = bank("ob", 2)
-            t = state["ob", b, h]
+            codes, scales = p_words(b, h)
+            quantise(
+                codes[:, 256 * n2 : 256 * n2 + 256],
+                scales[:, 256 * n2 : 256 * n2 + 256],
+                state["gp", b, h][:, 1024 * n2 : 1024 * n2 + 1024],
+            )
+
+        def s2(b, n, alone=False):
+            h, n2 = divmod(n, 2)
+            if alone:
+                t = bank("xt", 2)
+                state["ot", b, n] = t
+            else:
+                if n2 == 0:
+                    state["ob", b, h] = bank("ob", 2)
+                t = state["ob", b, h]
             for w in range(2):
-                col = 256 * (1 - w) + 128 * n2
-                pc = 128 * (2 * w + n2)
+                col = 128 * (1 - w) if alone else 256 * (1 - w) + 128 * n2
+                pc = 128 * (2 * n2 + w)
                 nc.tensor.matmul_mx(
                     out=t[:, col : col + 128],
                     lhsT=xq[b][:, 128 * n : 128 * n + 128].bitcast(FP8X4),
@@ -166,63 +192,95 @@ def tile_merge_mixtralsparsemoeblock_pa_t_kernel(tc, x, Wmean1, Wmean3, du1, dv1
             nc.scalar.activation(out=sg[:], in_=t[:, 0:256], func=ACT.Silu)
             nc.vector.tensor_tensor(out=z[b][:, 256 * h : 256 * h + 256], in0=sg[:], in1=t[:, 256:512], op=ALU.mult)
 
-        tx(0)
-        cx(0, 0, "act")
-        cx(0, 1, "dve")
-        for w in range(2):
+        def finish_tile(b, n):
+            t = state["ot", b, n]
+            sg = work.tile([P, 128], F32, name="sgt", tag="sgt", bufs=2)
+            nc.scalar.activation(out=sg[:], in_=t[:, 0:128], func=ACT.Silu)
+            nc.vector.tensor_tensor(out=z[b][:, 128 * n : 128 * n + 128], in0=sg[:], in1=t[:, 128:256], op=ALU.mult)
+
+        def store(b, c0, c1):
+            nc.sync.dma_start(out=out_blocks[b][:, c0:c1], in_=z[b][:, c0:c1])
+
+        def dv_transposes(w):
             df = dv_sb[w][:].bitcast(F32)
             for h in range(2):
                 state["dt", w, h] = transpose4(
                     "pb", 4, [df[:, 512 * h + 128 * k : 512 * h + 128 * k + 128] for k in range(4)]
                 )
-            interleave("act", gd[w][:, 0:1024], state["dt", w, 0])
-            interleave("dve" if w == 0 else "act", gd[w][:, 1024:2048], state["dt", w, 1])
-            if w == 0:
-                qx(0)
-            else:
-                quantise(dvq[0], dvs[0], gd[0])
-        tx(1)
-        cx(1, 0, "act")
-        cx(1, 1, "dve")
-        quantise(dvq[1], dvs[1], gd[1])
+
+        dv_transposes(0)
+        interleave("act", gd[0][:, 0:1024], state["dt", 0, 0])
+        interleave("dve", gd[0][:, 1024:2048], state["dt", 0, 1])
+        tx(0)
+        quantise(dvq[0][:], dvs[0][:], gd[0][:])
+        cx(0, 0, "act")
+        qx_half(0, 0)
+        cx(0, 1, "act")
+        qx_half(0, 1)
+        dv_transposes(1)
+        interleave("act", gd[1][:, 0:1024], state["dt", 1, 0])
+        interleave("dve", gd[1][:, 1024:2048], state["dt", 1, 1])
+        quantise(dvq[1][:], dvs[1][:], gd[1][:])
+        for n in range(4):
+            s1(0, n, 0)
+            cp(0, n, 0, "dve" if n % 2 == 1 else "act")
         wt = transpose4("ob", 2, [wm_sb[w][:].bitcast(F32)[:, 128 * u : 128 * u + 128] for w in range(2) for u in range(2)])
         ut = transpose4(
             "ob", 2,
             [du_sb[w][:].bitcast(F32).rearrange("i (m u) -> i u m", u=2)[:, u, :] for w in range(2) for u in range(2)],
         )
+        tx(1)
         interleave("act", gw[:, 0:1024], wt)
         interleave("act", gw[:, 1024:2048], ut)
+        cx(1, 0, "dve")
+        cx(1, 1, "act")
         qx(1)
-        quantise(wq, ws, gw)
+        quantise(wq[:], ws[:], gw[:])
+        for n in range(4):
+            s1(0, n, 1)
+            cp(0, n, 1, "dve" if n == 2 else "act")
+            if n == 1:
+                qp(0, 0)
 
-        for b in range(NB + 1):
-            ahead = 1 <= b and b + 1 < NB
-            if ahead:
+        LAST = NB - 1
+        for b in range(1, NB):
+            if b < LAST:
                 tx(b + 1)
             if b >= 2:
                 finish(b - 2, 1)
-                nc.sync.dma_start(out=out_blocks[b - 2], in_=z[b - 2][:])
-            if ahead:
+                store(b - 2, 0, 512)
+            if b < LAST:
                 cx(b + 1, 0, "act")
                 cx(b + 1, 1, "dve")
-            if b >= 1:
-                qp(b - 1, 1)
-            if ahead:
+            qp(b - 1, 1)
+            if b < LAST:
                 qx(b + 1)
             for n in range(4):
-                if b < NB:
-                    s1(b, n, 0)
-                    cp(b, n, 0, "act")
-                    s1(b, n, 1)
-                    cp(b, n, 1, "dve" if n % 2 == 1 else "act")
-                if b >= 1:
+                s1(b, n, 0)
+                cp(b, n, 0, "act")
+                s1(b, n, 1)
+                cp(b, n, 1, "dve" if n % 2 == 1 else "act")
+                if b < LAST or n < 2:
                     s2(b - 1, n)
                 if n == 1:
-                    if b >= 1:
-                        finish(b - 1, 0)
-                    if b < NB:
+                    finish(b - 1, 0)
+                    if b < LAST:
                         qp(b, 0)
-                    else:
-                        nc.sync.dma_start(out=out_blocks[NB - 1][:, 0:256], in_=z[NB - 1][:, 0:256])
-        finish(NB - 1, 1)
-        nc.sync.dma_start(out=out_blocks[NB - 1][:, 256:512], in_=z[NB - 1][:, 256:512])
+                if b == LAST and n >= 1:
+                    qp_tile(b, n - 1)
+
+        s2(LAST - 1, 2)
+        s2(LAST - 1, 3)
+        qp_tile(LAST, 3)
+        s2(LAST, 0)
+        s2(LAST, 1)
+        finish(LAST - 1, 1)
+        store(LAST - 1, 0, 512)
+        s2(LAST, 2, alone=True)
+        finish(LAST, 0)
+        store(LAST, 0, 256)
+        s2(LAST, 3, alone=True)
+        finish_tile(LAST, 2)
+        store(LAST, 256, 384)
+        finish_tile(LAST, 3)
+        store(LAST, 384, 512)

@@ -56,6 +56,8 @@ def tile_merge_mixtralsparsemoeblock_pa_t_kernel(tc, x, Wmean1, Wmean3, du1, dv1
 
         ident = const.tile([P, P], F32, name="ident")
         masks.make_identity(nc, ident[:])
+        zeros = const.tile([P, 512], BF16, name="zeros")
+        nc.vector.memset(zeros[:], 0.0)
         warm_in = const.tile([P, 1], F32, name="warm_in")
         warm_out = const.tile([P, 1], F32, name="warm_out")
         nc.vector.memset(warm_in[:], 0.0)
@@ -90,13 +92,18 @@ def tile_merge_mixtralsparsemoeblock_pa_t_kernel(tc, x, Wmean1, Wmean3, du1, dv1
 
         state = {}
 
-        def tx(b):
+        def keep_clock(count):
+            for k in range(count):
+                nc.tensor.matmul(out=state["warm"][:], lhsT=zeros[:, 0:128], rhs=zeros[:], start=True, stop=True)
+
+        def tx(b, pads=(0, 0)):
             xf = x_sb[b][:].bitcast(F32)
             state["gx", b] = work.tile([P, 2048], BF16, name="gx", tag="gx", bufs=2, align_bytes=64)
             for h in range(2):
                 state["xt", b, h] = transpose4(
                     "xt", 2, [xf[:, 512 * h + 128 * k : 512 * h + 128 * k + 128] for k in range(4)]
                 )
+                keep_clock(pads[h])
 
         def cx(b, h, engine):
             interleave(engine, state["gx", b][:, 1024 * h : 1024 * h + 1024], state["xt", b, h])
@@ -201,23 +208,26 @@ def tile_merge_mixtralsparsemoeblock_pa_t_kernel(tc, x, Wmean1, Wmean3, du1, dv1
         def store(b, c0, c1):
             nc.sync.dma_start(out=out_blocks[b][:, c0:c1], in_=z[b][:, c0:c1])
 
-        def dv_transposes(w):
+        def dv_transposes(w, pads):
             df = dv_sb[w][:].bitcast(F32)
             for h in range(2):
                 state["dt", w, h] = transpose4(
                     "pb", 4, [df[:, 512 * h + 128 * k : 512 * h + 128 * k + 128] for k in range(4)]
                 )
+                keep_clock(pads[h])
 
-        dv_transposes(0)
+        state["warm"] = bank("ob", 2)
+        keep_clock(5)
+        dv_transposes(0, (1, 1))
         interleave("act", gd[0][:, 0:1024], state["dt", 0, 0])
         interleave("dve", gd[0][:, 1024:2048], state["dt", 0, 1])
-        tx(0)
+        tx(0, (1, 1))
         quantise(dvq[0][:], dvs[0][:], gd[0][:])
         cx(0, 0, "act")
         qx_half(0, 0)
         cx(0, 1, "act")
         qx_half(0, 1)
-        dv_transposes(1)
+        dv_transposes(1, (1, 0))
         interleave("act", gd[1][:, 0:1024], state["dt", 1, 0])
         interleave("dve", gd[1][:, 1024:2048], state["dt", 1, 1])
         quantise(dvq[1][:], dvs[1][:], gd[1][:])

@@ -36,7 +36,7 @@ def tile_merge_mixtralsparsemoeblock_pa_t_kernel(tc, x, Wmean1, Wmean3, du1, dv1
                 nc.vector.tensor_copy(out=dst, in_=src)
 
         def bank(tag, bufs):
-            return psum.tile([P, 512], F32, name=tag, tag=tag, bufs=bufs)
+            return psum.tile([P, 512], F32, name=tag, tag="ps", bufs=8)
 
         def transpose4(tag, bufs, sources):
             t = bank(tag, bufs)
@@ -56,8 +56,6 @@ def tile_merge_mixtralsparsemoeblock_pa_t_kernel(tc, x, Wmean1, Wmean3, du1, dv1
 
         ident = const.tile([P, P], F32, name="ident")
         masks.make_identity(nc, ident[:])
-        zeros = const.tile([P, 512], BF16, name="zeros")
-        nc.vector.memset(zeros[:], 0.0)
         warm_in = const.tile([P, 1], F32, name="warm_in")
         warm_out = const.tile([P, 1], F32, name="warm_out")
         nc.vector.memset(warm_in[:], 0.0)
@@ -92,18 +90,13 @@ def tile_merge_mixtralsparsemoeblock_pa_t_kernel(tc, x, Wmean1, Wmean3, du1, dv1
 
         state = {}
 
-        def keep_clock(count):
-            for k in range(count):
-                nc.tensor.matmul(out=state["warm"][:], lhsT=zeros[:, 0:128], rhs=zeros[:], start=True, stop=True)
-
-        def tx(b, pads=(0, 0)):
+        def tx(b):
             xf = x_sb[b][:].bitcast(F32)
             state["gx", b] = work.tile([P, 2048], BF16, name="gx", tag="gx", bufs=2, align_bytes=64)
             for h in range(2):
                 state["xt", b, h] = transpose4(
                     "xt", 2, [xf[:, 512 * h + 128 * k : 512 * h + 128 * k + 128] for k in range(4)]
                 )
-                keep_clock(pads[h])
 
         def cx(b, h, engine):
             interleave(engine, state["gx", b][:, 1024 * h : 1024 * h + 1024], state["xt", b, h])
@@ -208,26 +201,23 @@ def tile_merge_mixtralsparsemoeblock_pa_t_kernel(tc, x, Wmean1, Wmean3, du1, dv1
         def store(b, c0, c1):
             nc.sync.dma_start(out=out_blocks[b][:, c0:c1], in_=z[b][:, c0:c1])
 
-        def dv_transposes(w, pads):
+        def dv_transposes(w):
             df = dv_sb[w][:].bitcast(F32)
             for h in range(2):
                 state["dt", w, h] = transpose4(
                     "pb", 4, [df[:, 512 * h + 128 * k : 512 * h + 128 * k + 128] for k in range(4)]
                 )
-                keep_clock(pads[h])
 
-        state["warm"] = bank("ob", 2)
-        keep_clock(5)
-        dv_transposes(0, (1, 1))
+        dv_transposes(0)
         interleave("act", gd[0][:, 0:1024], state["dt", 0, 0])
         interleave("dve", gd[0][:, 1024:2048], state["dt", 0, 1])
-        tx(0, (1, 1))
+        tx(0)
         quantise(dvq[0][:], dvs[0][:], gd[0][:])
         cx(0, 0, "act")
         qx_half(0, 0)
         cx(0, 1, "act")
         qx_half(0, 1)
-        dv_transposes(1, (1, 0))
+        dv_transposes(1)
         interleave("act", gd[1][:, 0:1024], state["dt", 1, 0])
         interleave("dve", gd[1][:, 1024:2048], state["dt", 1, 1])
         quantise(dvq[1][:], dvs[1][:], gd[1][:])

@@ -56,6 +56,8 @@ def tile_merge_mixtralsparsemoeblock_pa_t_kernel(tc, x, Wmean1, Wmean3, du1, dv1
 
         ident = const.tile([P, P], F32, name="ident")
         masks.make_identity(nc, ident[:])
+        zeros = const.tile([P, 512], BF16, name="zeros")
+        nc.vector.memset(zeros[:], 0.0)
         warm_in = const.tile([P, 1], F32, name="warm_in")
         warm_out = const.tile([P, 1], F32, name="warm_out")
         nc.vector.memset(warm_in[:], 0.0)
@@ -90,13 +92,18 @@ def tile_merge_mixtralsparsemoeblock_pa_t_kernel(tc, x, Wmean1, Wmean3, du1, dv1
 
         state = {}
 
-        def tx(b):
+        def keep_clock(count):
+            for k in range(count):
+                nc.tensor.matmul(out=state["warm"][:], lhsT=zeros[:, 0:128], rhs=zeros[:], start=True, stop=True)
+
+        def tx(b, pads=(0, 0)):
             xf = x_sb[b][:].bitcast(F32)
-            state["gx", b] = work.tile([P, 2048], BF16, name="gx", tag="gx", bufs=2, align_bytes=64)
+            state["gx", b] = work.tile([P, 2048], BF16, name="gx", tag="gx", bufs=4, align_bytes=64)
             for h in range(2):
                 state["xt", b, h] = transpose4(
                     "xt", 2, [xf[:, 512 * h + 128 * k : 512 * h + 128 * k + 128] for k in range(4)]
                 )
+                keep_clock(pads[h])
 
         def cx(b, h, engine):
             interleave(engine, state["gx", b][:, 1024 * h : 1024 * h + 1024], state["xt", b, h])
@@ -164,18 +171,19 @@ def tile_merge_mixtralsparsemoeblock_pa_t_kernel(tc, x, Wmean1, Wmean3, du1, dv1
                 if n2 == 0:
                     state["ob", b, h] = bank("ob", 2)
                 t = state["ob", b, h]
+            c0 = 0 if alone else 256 * n2
+            nc.tensor.matmul_mx(
+                out=t[:, c0 : c0 + 256],
+                lhsT=xq[b][:, 128 * n : 128 * n + 128].bitcast(FP8X4),
+                lhsT_scale=xs[b][:, 128 * n : 128 * n + 128],
+                rhs=wq[:, 0:256].bitcast(FP8X4),
+                rhs_scale=ws[:, 0:256],
+                start=True,
+                stop=False,
+            )
             for w in range(2):
-                col = 128 * (1 - w) if alone else 256 * (1 - w) + 128 * n2
+                col = c0 + 128 * w
                 pc = 128 * (2 * n2 + w)
-                nc.tensor.matmul_mx(
-                    out=t[:, col : col + 128],
-                    lhsT=xq[b][:, 128 * n : 128 * n + 128].bitcast(FP8X4),
-                    lhsT_scale=xs[b][:, 128 * n : 128 * n + 128],
-                    rhs=wq[:, 128 * w : 128 * w + 128].bitcast(FP8X4),
-                    rhs_scale=ws[:, 128 * w : 128 * w + 128],
-                    start=True,
-                    stop=False,
-                )
                 nc.tensor.matmul_mx(
                     out=t[:, col : col + 128],
                     lhsT=state["pq", b, h][:, pc : pc + 128].bitcast(FP8X4),
@@ -183,41 +191,48 @@ def tile_merge_mixtralsparsemoeblock_pa_t_kernel(tc, x, Wmean1, Wmean3, du1, dv1
                     rhs=wq[:, 256 + 128 * w : 256 + 128 * w + 128].bitcast(FP8X4),
                     rhs_scale=ws[:, 256 + 128 * w : 256 + 128 * w + 128],
                     start=False,
-                    stop=True,
+                    stop=(w == 1),
                 )
 
         def finish(b, h):
             t = state["ob", b, h]
             sg = work.tile([P, 256], F32, name="sg", tag="sg", bufs=3)
-            nc.scalar.activation(out=sg[:], in_=t[:, 0:256], func=ACT.Silu)
-            nc.vector.tensor_tensor(out=z[b][:, 256 * h : 256 * h + 256], in0=sg[:], in1=t[:, 256:512], op=ALU.mult)
+            tv = t[:].rearrange("p (n g i) -> p n g i", n=2, g=2)
+            sv = sg[:].rearrange("p (n i) -> p n i", n=2)
+            nc.scalar.activation(out=sv, in_=tv[:, :, 1, :], func=ACT.Silu)
+            nc.vector.tensor_tensor(
+                out=z[b][:, 256 * h : 256 * h + 256].rearrange("p (n i) -> p n i", n=2), in0=sv, in1=tv[:, :, 0, :], op=ALU.mult
+            )
 
         def finish_tile(b, n):
             t = state["ot", b, n]
             sg = work.tile([P, 128], F32, name="sgt", tag="sgt", bufs=2)
-            nc.scalar.activation(out=sg[:], in_=t[:, 0:128], func=ACT.Silu)
-            nc.vector.tensor_tensor(out=z[b][:, 128 * n : 128 * n + 128], in0=sg[:], in1=t[:, 128:256], op=ALU.mult)
+            nc.scalar.activation(out=sg[:], in_=t[:, 128:256], func=ACT.Silu)
+            nc.vector.tensor_tensor(out=z[b][:, 128 * n : 128 * n + 128], in0=sg[:], in1=t[:, 0:128], op=ALU.mult)
 
         def store(b, c0, c1):
             nc.sync.dma_start(out=out_blocks[b][:, c0:c1], in_=z[b][:, c0:c1])
 
-        def dv_transposes(w):
+        def dv_transposes(w, pads):
             df = dv_sb[w][:].bitcast(F32)
             for h in range(2):
                 state["dt", w, h] = transpose4(
                     "pb", 4, [df[:, 512 * h + 128 * k : 512 * h + 128 * k + 128] for k in range(4)]
                 )
+                keep_clock(pads[h])
 
-        dv_transposes(0)
+        state["warm"] = bank("ob", 2)
+        keep_clock(5)
+        dv_transposes(0, (1, 1))
         interleave("act", gd[0][:, 0:1024], state["dt", 0, 0])
         interleave("dve", gd[0][:, 1024:2048], state["dt", 0, 1])
-        tx(0)
+        tx(0, (1, 1))
         quantise(dvq[0][:], dvs[0][:], gd[0][:])
         cx(0, 0, "act")
         qx_half(0, 0)
         cx(0, 1, "act")
         qx_half(0, 1)
-        dv_transposes(1)
+        dv_transposes(1, (1, 0))
         interleave("act", gd[1][:, 0:1024], state["dt", 1, 0])
         interleave("dve", gd[1][:, 1024:2048], state["dt", 1, 1])
         quantise(dvq[1][:], dvs[1][:], gd[1][:])
@@ -244,17 +259,22 @@ def tile_merge_mixtralsparsemoeblock_pa_t_kernel(tc, x, Wmean1, Wmean3, du1, dv1
 
         LAST = NB - 1
         for b in range(1, NB):
-            if b < LAST:
+            pair = b % 2 == 1 and b < LAST
+            if pair:
                 tx(b + 1)
+                tx(b + 2)
             if b >= 2:
                 finish(b - 2, 1)
                 store(b - 2, 0, 512)
-            if b < LAST:
+            if pair:
                 cx(b + 1, 0, "act")
                 cx(b + 1, 1, "dve")
             qp(b - 1, 1)
             if b < LAST:
                 qx(b + 1)
+            if pair:
+                cx(b + 2, 0, "act")
+                cx(b + 2, 1, "dve")
             for n in range(4):
                 s1(b, n, 0)
                 cp(b, n, 0, "act")

from contextlib import ExitStack

import concourse.masks as masks
import concourse.mybir as mybir

F32 = mybir.dt.float32
BF16 = mybir.dt.bfloat16
U32 = mybir.dt.uint32
U8 = mybir.dt.uint8
FP8X4 = mybir.dt.float8_e4m3fn_x4
ACT = mybir.ActivationFunctionType
ALU = mybir.AluOpType

T, H, I, R = 4096, 512, 128, 512
P = 128
BLOCK = 512
NB = T // BLOCK
FLOPS = 2 * T * (2 * H * R + 2 * H * I + 2 * R * I)


def tile_merge_mixtralsparsemoeblock_pa_t_kernel(tc, x, Wmean1, Wmean3, du1, dv1, du3, dv3, out):
    nc = tc.nc
    x_blocks = x.rearrange("(b p n) h -> b p (n h)", p=P, n=4)
    out_blocks = out.rearrange("(b p n) i -> b p (n i)", p=P, n=4)

    with ExitStack() as ctx:
        const = ctx.enter_context(tc.tile_pool(name="const", bufs=1))
        work = ctx.enter_context(tc.tile_pool(name="work", bufs=2))
        psum = ctx.enter_context(tc.psum_pool(name="psum", bufs=2))
        ctx.enter_context(tc.manual_schedule())

        def copy_on(engine, dst, src):
            if engine == "act":
                nc.scalar.copy(out=dst, in_=src)
            else:
                nc.vector.tensor_copy(out=dst, in_=src)

        def bank(tag, bufs):
            return psum.tile([P, 512], F32, name=tag, tag="ps", bufs=8)

        def transpose4(tag, bufs, sources):
            t = bank(tag, bufs)
            for k, src in enumerate(sources):
                nc.tensor.transpose(t[:, 128 * k : 128 * k + 128], src, ident[:])
            return t

        def interleave(engine, dst_bf16, t):
            copy_on(
                engine,
                dst_bf16.bitcast(F32).rearrange("q (a c u) -> q a c u", a=2, u=2),
                t[:].rearrange("q (a u c) -> q a c u", a=2, u=2),
            )

        def quantise(codes, scales, src):
            nc.vector.quantize_mx(out=codes.bitcast(FP8X4), scales=scales, in_=src)

        ident = const.tile([P, P], F32, name="ident")
        masks.make_identity(nc, ident[:])
        zeros = const.tile([P, 512], BF16, name="zeros")
        nc.vector.memset(zeros[:], 0.0)
        warm_in = const.tile([P, 1], F32, name="warm_in")
        warm_out = const.tile([P, 1], F32, name="warm_out")
        nc.vector.memset(warm_in[:], 0.0)
        nc.scalar.activation(out=warm_out[:], in_=warm_in[:], func=ACT.Silu)

        x_sb = [const.tile([P, 2048], BF16, name="x_sb%d" % b) for b in range(NB)]
        dv_sb = [const.tile([P, 2048], BF16, name="dv_sb%d" % w) for w in range(2)]
        wm_sb = [const.tile([P, 512], BF16, name="wm_sb%d" % w) for w in range(2)]
        du_sb = [const.tile([P, 512], BF16, name="du_sb%d" % w) for w in range(2)]
        dv3_rows = dv3.rearrange("(m j) h -> m (j h)", j=4)
        nc.sync.dma_start(out=dv_sb[0][:, 0:1024], in_=dv3_rows[:, 0:1024])
        nc.sync.dma_start(out=dv_sb[0][:, 1024:2048], in_=dv3_rows[:, 1024:2048])
        nc.sync.dma_start(out=x_sb[0][:, 0:1024], in_=x_blocks[0][:, 0:1024])
        nc.sync.dma_start(out=x_sb[0][:, 1024:2048], in_=x_blocks[0][:, 1024:2048])
        nc.sync.dma_start(out=dv_sb[1][:], in_=dv1.rearrange("(m j) h -> m (j h)", j=4))
        nc.sync.dma_start(out=wm_sb[0][:], in_=Wmean3)
        nc.sync.dma_start(out=wm_sb[1][:], in_=Wmean1)
        nc.sync.dma_start(out=du_sb[0][:], in_=du3)
        nc.sync.dma_start(out=du_sb[1][:], in_=du1)
        for b in range(1, NB):
            nc.sync.dma_start(out=x_sb[b][:], in_=x_blocks[b])

        xq = [const.tile([P, 512], U32, name="xq%d" % b, align_bytes=64) for b in range(NB)]
        xs = [const.tile([P, 512], U8, name="xs%d" % b, align_bytes=64) for b in range(NB)]
        dvq = [const.tile([P, 512], U32, name="dvq%d" % w, align_bytes=64) for w in range(2)]
        dvs = [const.tile([P, 512], U8, name="dvs%d" % w, align_bytes=64) for w in range(2)]
        gd = [const.tile([P, 2048], BF16, name="gd%d" % w, align_bytes=64) for w in range(2)]
        gw = const.tile([P, 2048], BF16, name="gw", align_bytes=64)
        wq = const.tile([P, 512], U32, name="wq", align_bytes=64)
        ws = const.tile([P, 512], U8, name="ws", align_bytes=64)
        z = [const.tile([P, 512], F32, name="z%d" % b) for b in range(NB)]

        state = {}

        def keep_clock(count):
            for k in range(count):
                nc.tensor.matmul(out=state["warm"][:], lhsT=zeros[:, 0:128], rhs=zeros[:], start=True, stop=True)

        def tx(b, pads=(0, 0)):
            xf = x_sb[b][:].bitcast(F32)
            state["gx", b] = work.tile([P, 2048], BF16, name="gx", tag="gx", bufs=4, align_bytes=64)
            for h in range(2):
                state["xt", b, h] = transpose4(
                    "xt", 2, [xf[:, 512 * h + 128 * k : 512 * h + 128 * k + 128] for k in range(4)]
                )
                keep_clock(pads[h])

        def cx(b, h, engine):
            interleave(engine, state["gx", b][:, 1024 * h : 1024 * h + 1024], state["xt", b, h])

        def qx(b):
            quantise(xq[b][:], xs[b][:], state["gx", b][:])

        def qx_half(b, h):
            quantise(
                xq[b][:, 256 * h : 256 * h + 256],
                xs[b][:, 256 * h : 256 * h + 256],
                state["gx", b][:, 1024 * h : 1024 * h + 1024],
            )

        def s1(b, n, w):
            t = bank("pb", 4)
            state["pb", b, n, w] = t
            for j in range(4):
                nc.tensor.matmul_mx(
                    out=t[:, 128 * j : 128 * j + 128],
                    lhsT=dvq[w][:, 128 * j : 128 * j + 128].bitcast(FP8X4),
                    lhsT_scale=dvs[w][:, 128 * j : 128 * j + 128],
                    rhs=xq[b][:, 128 * n : 128 * n + 128].bitcast(FP8X4),
                    rhs_scale=xs[b][:, 128 * n : 128 * n + 128],
                    start=True,
                    stop=True,
                )

        def cp(b, n, w, engine):
            h, n2 = divmod(n, 2)
            if ("gp", b, h) not in state:
                state["gp", b, h] = work.tile([P, 2048], BF16, name="gp", tag="gp", bufs=4, align_bytes=64)
            c = 512 * (2 * n2 + w)
            copy_on(
                engine,
                state["gp", b, h][:, c : c + 512].rearrange("m (t j) -> m t j", j=4),
                state["pb", b, n, w][:].rearrange("m (j t) -> m t j", j=4),
            )

        def p_words(b, h):
            if ("pq", b, h) not in state:
                state["pq", b, h] = work.tile([P, 512], U32, name="pq", tag="pq", bufs=4, align_bytes=64)
                state["ps", b, h] = work.tile([P, 512], U8, name="ps", tag="ps", bufs=4, align_bytes=64)
            return state["pq", b, h], state["ps", b, h]

        def qp(b, h):
            codes, scales = p_words(b, h)
            quantise(codes[:], scales[:], state["gp", b, h][:])

        def qp_tile(b, n):
            h, n2 = divmod(n, 2)
            codes, scales = p_words(b, h)
            quantise(
                codes[:, 256 * n2 : 256 * n2 + 256],
                scales[:, 256 * n2 : 256 * n2 + 256],
                state["gp", b, h][:, 1024 * n2 : 1024 * n2 + 1024],
            )

        def s2(b, n, alone=False):
            h, n2 = divmod(n, 2)
            if alone:
                t = bank("xt", 2)
                state["ot", b, n] = t
            else:
                if n2 == 0:
                    state["ob", b, h] = bank("ob", 2)
                t = state["ob", b, h]
            c0 = 0 if alone else 256 * n2
            nc.tensor.matmul_mx(
                out=t[:, c0 : c0 + 256],
                lhsT=xq[b][:, 128 * n : 128 * n + 128].bitcast(FP8X4),
                lhsT_scale=xs[b][:, 128 * n : 128 * n + 128],
                rhs=wq[:, 0:256].bitcast(FP8X4),
                rhs_scale=ws[:, 0:256],
                start=True,
                stop=False,
            )
            for w in range(2):
                col = c0 + 128 * w
                pc = 128 * (2 * n2 + w)
                nc.tensor.matmul_mx(
                    out=t[:, col : col + 128],
                    lhsT=state["pq", b, h][:, pc : pc + 128].bitcast(FP8X4),
                    lhsT_scale=state["ps", b, h][:, pc : pc + 128],
                    rhs=wq[:, 256 + 128 * w : 256 + 128 * w + 128].bitcast(FP8X4),
                    rhs_scale=ws[:, 256 + 128 * w : 256 + 128 * w + 128],
                    start=False,
                    stop=(w == 1),
                )

        def finish(b, h):
            t = state["ob", b, h]
            sg = work.tile([P, 256], F32, name="sg", tag="sg", bufs=3)
            tv = t[:].rearrange("p (n g i) -> p n g i", n=2, g=2)
            sv = sg[:].rearrange("p (n i) -> p n i", n=2)
            nc.scalar.activation(out=sv, in_=tv[:, :, 1, :], func=ACT.Silu)
            nc.vector.tensor_tensor(
                out=z[b][:, 256 * h : 256 * h + 256].rearrange("p (n i) -> p n i", n=2), in0=sv, in1=tv[:, :, 0, :], op=ALU.mult
            )

        def finish_tile(b, n):
            t = state["ot", b, n]
            sg = work.tile([P, 128], F32, name="sgt", tag="sgt", bufs=2)
            nc.scalar.activation(out=sg[:], in_=t[:, 128:256], func=ACT.Silu)
            nc.vector.tensor_tensor(out=z[b][:, 128 * n : 128 * n + 128], in0=sg[:], in1=t[:, 0:128], op=ALU.mult)

        def store(b, c0, c1):
            nc.sync.dma_start(out=out_blocks[b][:, c0:c1], in_=z[b][:, c0:c1])

        def dv_transposes(w, pads):
            df = dv_sb[w][:].bitcast(F32)
            for h in range(2):
                state["dt", w, h] = transpose4(
                    "pb", 4, [df[:, 512 * h + 128 * k : 512 * h + 128 * k + 128] for k in range(4)]
                )
                keep_clock(pads[h])

        state["warm"] = bank("ob", 2)
        keep_clock(5)
        dv_transposes(0, (1, 1))
        interleave("act", gd[0][:, 0:1024], state["dt", 0, 0])
        interleave("dve", gd[0][:, 1024:2048], state["dt", 0, 1])
        tx(0, (1, 1))
        quantise(dvq[0][:], dvs[0][:], gd[0][:])
        cx(0, 0, "act")
        qx_half(0, 0)
        cx(0, 1, "act")
        qx_half(0, 1)
        dv_transposes(1, (1, 0))
        interleave("act", gd[1][:, 0:1024], state["dt", 1, 0])
        interleave("dve", gd[1][:, 1024:2048], state["dt", 1, 1])
        quantise(dvq[1][:], dvs[1][:], gd[1][:])
        for n in range(4):
            s1(0, n, 0)
            cp(0, n, 0, "dve" if n % 2 == 1 else "act")
        wt = transpose4("ob", 2, [wm_sb[w][:].bitcast(F32)[:, 128 * u : 128 * u + 128] for w in range(2) for u in range(2)])
        ut = transpose4(
            "ob", 2,
            [du_sb[w][:].bitcast(F32).rearrange("i (m u) -> i u m", u=2)[:, u, :] for w in range(2) for u in range(2)],
        )
        tx(1)
        interleave("act", gw[:, 0:1024], wt)
        interleave("act", gw[:, 1024:2048], ut)
        cx(1, 0, "dve")
        cx(1, 1, "act")
        qx(1)
        quantise(wq[:], ws[:], gw[:])
        for n in range(4):
            s1(0, n, 1)
            cp(0, n, 1, "dve" if n == 2 else "act")
            if n == 1:
                qp(0, 0)

        LAST = NB - 1
        for b in range(1, NB):
            pair = b % 2 == 1 and b < LAST
            if pair:
                tx(b + 1)
                tx(b + 2)
            if b >= 2:
                finish(b - 2, 1)
                store(b - 2, 0, 512)
            if pair:
                cx(b + 1, 0, "act")
                cx(b + 1, 1, "dve")
            qp(b - 1, 1)
            if b < LAST:
                qx(b + 1)
            if pair:
                cx(b + 2, 0, "act")
                cx(b + 2, 1, "dve")
            for n in range(4):
                s1(b, n, 0)
                cp(b, n, 0, "act")
                s1(b, n, 1)
                cp(b, n, 1, "dve" if n % 2 == 1 else "act")
                if b < LAST or n < 2:
                    s2(b - 1, n)
                if n == 1:
                    finish(b - 1, 0)
                    if b < LAST:
                        qp(b, 0)
                if b == LAST and n >= 1:
                    qp_tile(b, n - 1)

        s2(LAST - 1, 2)
        s2(LAST - 1, 3)
        qp_tile(LAST, 3)
        s2(LAST, 0)
        s2(LAST, 1)
        finish(LAST - 1, 1)
        store(LAST - 1, 0, 512)
        s2(LAST, 2, alone=True)
        finish(LAST, 0)
        store(LAST, 0, 256)
        s2(LAST, 3, alone=True)
        finish_tile(LAST, 2)
        store(LAST, 256, 384)
        finish_tile(LAST, 3)
        store(LAST, 384, 512)
